import numpy as np
import ml_dtypes


def mxq(x, axis, fmt="e4m3"):
    dtype, down = {"e4m3": (ml_dtypes.float8_e4m3fn, 7), "e5m2": (ml_dtypes.float8_e5m2, 14)}[fmt]
    v = np.moveaxis(np.asarray(x, np.float32).astype(ml_dtypes.bfloat16).astype(np.float64), axis, -1)
    blocks = v.reshape(v.shape[:-1] + (-1, 32))
    amax = np.abs(blocks).max(-1, keepdims=True)
    byte = np.maximum(np.where(amax > 0, np.frexp(amax)[1] - 1 + 127, 0) - down, 1)
    scale = np.exp2(byte - 127.0)
    codes = (blocks / scale).astype(np.float32).astype(dtype).astype(np.float64)
    return np.moveaxis((codes * scale).reshape(v.shape), -1, axis)


WIDE = False


def mx_kscale(k):
    if not WIDE:
        return np.ones(k)
    levels = np.array([10, -10, 5, -5, 0])
    a = np.random.permutation(np.resize(levels, k // 512 * 4)).reshape(k // 512, 4)
    idx = np.arange(k)
    return np.exp2(a[idx // 512, idx % 128 // 32])


BF16 = ml_dtypes.bfloat16


def bf(x):
    return np.asarray(x, np.float32).astype(BF16)


def f64(x):
    return np.asarray(x).astype(np.float64)


B, G, DB, DR = 512, 16, 512, 1024


def mish(v):
    return v * np.tanh(np.log(1.0 + np.exp(v)))


def setup_inputs():
    s, t = mx_kscale(DR), mx_kscale(DB)
    return {"BB_feature": bf(np.random.standard_normal((B, G, DB)) * t),
            "RF_feature": bf(np.random.standard_normal((B, DR)) * s),
            "W_bbbb": bf(np.random.standard_normal((DB, DB)) / np.sqrt(DB) / t),
            "b_bbbb": bf(np.random.standard_normal(DB) * 0.5),
            "W_rfbb": bf(np.random.standard_normal((DB, DR)) / np.sqrt(DR) / s),
            "b_rfbb": bf(np.random.standard_normal(DB) * 0.5)}


def reference(BB_feature, RF_feature, W_bbbb, b_bbbb, W_rfbb, b_rfbb):
    RF_to_BB = mish((mxq(f64(RF_feature), 1, "e4m3") @ mxq(f64(W_rfbb), 1, "e4m3").T) + f64(b_rfbb))
    BB_to_BB = mish((mxq(f64(BB_feature), 2, "e4m3") @ mxq(f64(W_bbbb), 1, "e4m3").T) + f64(b_bbbb))
    return BB_to_BB + RF_to_BB[:, None, :]

@@ -1,0 +1,263 @@
+from contextlib import ExitStack
+
+import concourse.mybir as mybir
+from concourse.masks import make_identity
+
+F32 = mybir.dt.float32
+BF16 = mybir.dt.bfloat16
+U32 = mybir.dt.uint32
+U8 = mybir.dt.uint8
+FP8X4 = mybir.dt.float8_e4m3fn_x4
+ACT = mybir.ActivationFunctionType
+ALU = mybir.AluOpType
+
+B, G, DB, DR = 512, 16, 512, 1024
+FLOPS = 2 * B * G * DB * DB + 2 * B * DR * DB
+
+P = 128
+PACK = 4
+K_PASS = P * PACK
+BLOCKS = 4
+CHUNK = BLOCKS * P
+HALF = BLOCKS // 2
+
+GROUP_SIZES = (10, 5, 2)
+
+LEAD = 3
+
+GUARD = 2.0 ** -60
+
+
+def tile_gnn_layer_pb_t_kernel(
+    tc, BB_feature, RF_feature, W_bbbb, b_bbbb, W_rfbb, b_rfbb, out
+):
+    nc = tc.nc
+    with ExitStack() as ctx:
+        consts = ctx.enter_context(tc.tile_pool(name="consts", bufs=1))
+        keep = ctx.enter_context(tc.tile_pool(name="keep", bufs=1))
+        raws = ctx.enter_context(tc.tile_pool(name="raws", bufs=4))
+        groupeds = ctx.enter_context(tc.tile_pool(name="groupeds", bufs=3))
+        acts = ctx.enter_context(tc.tile_pool(name="acts", bufs=13))
+        stages = ctx.enter_context(tc.tile_pool(name="stages", bufs=4))
+        front = ctx.enter_context(tc.psum_pool(name="front", bufs=4))
+        rest = ctx.enter_context(tc.psum_pool(name="rest", bufs=4))
+        ctx.enter_context(tc.manual_schedule())
+
+        ident = consts.tile([P, P], F32, name="ident")
+        make_identity(nc, ident[:])
+        guard = consts.tile([P, 1], F32, name="guard")
+        nc.vector.memset(guard[:], GUARD)
+        scratch = consts.tile([P, 1], F32, name="scratch")
+
+        def call_in_sigmoid_table():
+            nc.scalar.activation(out=scratch[:], in_=guard[:], func=ACT.Sigmoid)
+
+        call_in_sigmoid_table()
+
+        bias_rows = consts.tile([P, P], BF16, name="bias_rows")
+        nc.vector.memset(bias_rows[:], 0.0)
+        nc.sync.dma_start(
+            out=bias_rows[0:BLOCKS, :], in_=b_bbbb.rearrange("(o p) -> o p", p=P)
+        )
+        nc.sync.dma_start(
+            out=bias_rows[BLOCKS : 2 * BLOCKS, :], in_=b_rfbb.rearrange("(o p) -> o p", p=P)
+        )
+        bias_rows_f32 = consts.tile([P, P], F32, name="bias_rows_f32")
+        nc.vector.tensor_copy(out=bias_rows_f32[:], in_=bias_rows[:])
+        bias_bank = rest.tile([P, CHUNK], F32, name="bank")
+        nc.tensor.transpose(bias_bank[:, 0:P], bias_rows_f32[:], ident[:])
+        bias = consts.tile([P, 2 * BLOCKS], F32, name="bias")
+        nc.vector.tensor_copy(out=bias[:], in_=bias_bank[:, 0 : 2 * BLOCKS])
+        neg_bias = consts.tile([P, 2 * BLOCKS], F32, name="neg_bias")
+        nc.vector.tensor_scalar_mul(out=neg_bias[:], in0=bias[:], scalar1=-1.0)
+
+        rf_to_bb = consts.tile([P, BLOCKS, DB], F32, name="rf_to_bb")
+
+        def new_operand(label, passes):
+            codes = keep.tile([P, passes, CHUNK], U32, name="codes_" + label, align_bytes=64)
+            scales = keep.tile([P, passes, CHUNK], U8, name="scales_" + label, align_bytes=64)
+            return {"codes": codes, "scales": scales, "passes": passes}
+
+        def prepare(operand, c, rows, scalar_helps=False):
+            raw = raws.tile([P, BLOCKS, K_PASS], BF16, name="raw")
+            nc.sync.dma_start(out=raw[:], in_=rows)
+            words = raw[:].bitcast(F32)
+            grouped = groupeds.tile([P, CHUNK * PACK], BF16, name="grouped", align_bytes=64)
+            grouped_words = grouped[:].bitcast(F32).rearrange(
+                "p (j r u) -> p j r u", j=BLOCKS, u=2
+            )
+            for h in range(HALF):
+                bank = rest.tile([P, CHUNK], F32, name="bank")
+                flipped = bank[:].rearrange("p (j u r) -> p j u r", j=2, u=2)
+                for j in range(2):
+                    for u in range(2):
+                        nc.tensor.transpose(
+                            flipped[:, j, u, :],
+                            words[:, 2 * h + j, u * P : (u + 1) * P],
+                            ident[:],
+                        )
+                copy = nc.scalar.copy if scalar_helps and h == 1 else nc.vector.tensor_copy
+                copy(
+                    out=grouped_words[:, 2 * h : 2 * h + 2, :, :],
+                    in_=flipped.rearrange("p j u r -> p j r u"),
+                )
+            nc.vector.quantize_mx(
+                out=operand["codes"][:, c, :].bitcast(FP8X4),
+                scales=operand["scales"][:, c, :],
+                in_=grouped[:],
+            )
+
+        def product(bank, chunk, o):
+            w, x = chunk["w"], chunk["x"]
+            cols = slice(o * P, (o + 1) * P)
+            for c in range(x["passes"]):
+                nc.tensor.matmul_mx(
+                    out=bank[:],
+                    lhsT=w["codes"][:, c, cols].bitcast(FP8X4),
+                    lhsT_scale=w["scales"][:, c, cols],
+                    rhs=x["codes"][:, c, :].bitcast(FP8X4),
+                    rhs_scale=x["scales"][:, c, :],
+                    start=(c == 0),
+                    stop=(c == x["passes"] - 1),
+                )
+
+        def sigmoid(chunk):
+            act = acts.tile([P, BLOCKS, CHUNK], F32, name="act")
+            chunk["act"] = act
+            for o in range(BLOCKS):
+                bank = front.tile([P, CHUNK], F32, name="first")
+                product(bank, chunk, o)
+                col = chunk["bias"] + o
+                nc.scalar.activation(
+                    out=act[:, o, :],
+                    in_=bank[:],
+                    func=ACT.Sigmoid,
+                    bias=neg_bias[:, col : col + 1],
+                    scale=-1.0,
+                )
+
+        def log(chunk):
+            act = chunk["act"]
+            nc.scalar.activation(
+                out=act[:], in_=act[:], func=ACT.Ln, bias=guard[:, 0:1], scale=1.0
+            )
+
+        def tanh(chunk):
+            act = chunk["act"]
+            for h in range(HALF):
+                half = act[:, 2 * h : 2 * h + 2, :]
+                nc.scalar.activation(out=half, in_=half, func=ACT.Tanh, scale=-1.0)
+
+        def times_z(chunk, h):
+            act = chunk["act"]
+            for o in range(2 * h, 2 * h + 2):
+                bank = rest.tile([P, CHUNK], F32, name="bank")
+                product(bank, chunk, o)
+                col = chunk["bias"] + o
+                nc.vector.scalar_tensor_tensor(
+                    out=act[:, o, :],
+                    in0=bank[:],
+                    scalar=bias[:, col : col + 1],
+                    in1=act[:, o, :],
+                    op0=ALU.add,
+                    op1=ALU.mult,
+                )
+
+        def turn_back(chunk, h):
+            act = chunk["act"]
+            stage = None
+            if chunk["sample_block"] is not None:
+                stage = stages.tile([P, 2, DB], F32, name="stage")
+            for j in range(2 * h, 2 * h + 2):
+                bank = rest.tile([P, CHUNK], F32, name="bank")
+                for o in range(BLOCKS):
+                    nc.tensor.transpose(
+                        bank[:, o * P : (o + 1) * P], act[:, o, j * P : (j + 1) * P], ident[:]
+                    )
+                if chunk["sample_block"] is None:
+                    nc.vector.tensor_copy(out=rf_to_bb[:, j, :], in_=bank[:])
+                else:
+                    nc.vector.tensor_tensor(
+                        out=stage[:, j - 2 * h, :],
+                        in0=bank[:],
+                        in1=rf_to_bb[:, chunk["sample_block"], :],
+                        op=ALU.add,
+                    )
+            if chunk["sample_block"] is not None:
+                s, g0 = chunk["sample_block"], chunk["first_group"] + 2 * h
+                nc.sync.dma_start(out=out[s * P : (s + 1) * P, g0 : g0 + 2, :], in_=stage[:])
+
+        w_bb = new_operand("w_bb", 1)
+        w_rf = new_operand("w_rf", DR // K_PASS)
+        x_rf = new_operand("x_rf", DR // K_PASS)
+        w_bb_rows = W_bbbb.rearrange("(j p) k -> p j k", p=P)
+        w_rf_rows = W_rfbb.rearrange("(j p) k -> p j k", p=P)
+        x_rf_rows = RF_feature.rearrange("(j p) k -> p j k", p=P)
+
+        rf_chunk = {"x": x_rf, "w": w_rf, "bias": BLOCKS, "sample_block": None}
+        rf_passes = []
+        for c in range(DR // K_PASS):
+            k_cols = slice(c * K_PASS, (c + 1) * K_PASS)
+            rf_passes.append((w_rf, c, w_rf_rows[:, :, k_cols]))
+            rf_passes.append((x_rf, c, x_rf_rows[:, :, k_cols]))
+
+        bb_chunks = []
+        for n in range(B * G // CHUNK):
+            s, g0 = n // (G // BLOCKS), BLOCKS * (n % (G // BLOCKS))
+            bb_chunks.append(
+                {
+                    "x": new_operand("x_bb%d" % n, 1),
+                    "w": w_bb,
+                    "bias": 0,
+                    "sample_block": s,
+                    "first_group": g0,
+                }
+            )
+
+        def bb_pass(chunk):
+            s, g0 = chunk["sample_block"], chunk["first_group"]
+            return (chunk["x"], 0, BB_feature[s * P : (s + 1) * P, g0 : g0 + BLOCKS, :])
+
+        n_first = GROUP_SIZES[0] - 1
+        groups = [[rf_chunk] + bb_chunks[:n_first]]
+        start = n_first
+        for size in GROUP_SIZES[1:]:
+            groups.append(bb_chunks[start : start + size])
+            start += size
+        assert start == len(bb_chunks)
+
+        passes = [(w_bb, 0, w_bb_rows)]
+        passes.extend([bb_pass(chunk) for chunk in bb_chunks[:n_first]])
+        passes.extend(rf_passes)
+        passes.extend([bb_pass(chunk) for chunk in bb_chunks[n_first:]])
+
+        def written_before(i):
+            return min(len(passes), LEAD + i + i // 3)
+
+        done = 0
+        for i, chunk in enumerate(bb_chunks[:n_first] + [rf_chunk]):
+            for k in range(done, written_before(i)):
+                prepare(*passes[k], scalar_helps=(k < 2))
+            done = written_before(i)
+            sigmoid(chunk)
+        assert done >= 1 + n_first + len(rf_passes)
+        for k in range(done, len(passes)):
+            prepare(*passes[k])
+
+        for g, group in enumerate(groups):
+            following = groups[g + 1] if g + 1 < len(groups) else []
+            for chunk in group:
+                log(chunk)
+            call_in_sigmoid_table()
+            previous = None
+            for i, chunk in enumerate(group):
+                tanh(chunk)
+                if i < len(following):
+                    sigmoid(following[i])
+                for h in range(HALF):
+                    times_z(chunk, h)
+                    if previous is not None:
+                        turn_back(previous, h)
+                previous = chunk
+            for h in range(HALF):
+                turn_back(previous, h)

@@ -23,7 +23,7 @@ HALF = BLOCKS // 2
 
 GROUP_SIZES = (10, 5, 2)
 
-LEAD = 3
+LEAD = 4
 
 GUARD = 2.0 ** -60
 
@@ -36,9 +36,9 @@ def tile_gnn_layer_pb_t_kernel(
         consts = ctx.enter_context(tc.tile_pool(name="consts", bufs=1))
         keep = ctx.enter_context(tc.tile_pool(name="keep", bufs=1))
         raws = ctx.enter_context(tc.tile_pool(name="raws", bufs=4))
-        groupeds = ctx.enter_context(tc.tile_pool(name="groupeds", bufs=3))
+        groupeds = ctx.enter_context(tc.tile_pool(name="groupeds", bufs=4))
         acts = ctx.enter_context(tc.tile_pool(name="acts", bufs=13))
-        stages = ctx.enter_context(tc.tile_pool(name="stages", bufs=4))
+        stages = ctx.enter_context(tc.tile_pool(name="stages", bufs=8))
         front = ctx.enter_context(tc.psum_pool(name="front", bufs=4))
         rest = ctx.enter_context(tc.psum_pool(name="rest", bufs=4))
         ctx.enter_context(tc.manual_schedule())
@@ -78,7 +78,7 @@ def tile_gnn_layer_pb_t_kernel(
             scales = keep.tile([P, passes, CHUNK], U8, name="scales_" + label, align_bytes=64)
             return {"codes": codes, "scales": scales, "passes": passes}
 
-        def prepare(operand, c, rows, scalar_helps=False):
+        def regroup(rows, scalar_helps):
             raw = raws.tile([P, BLOCKS, K_PASS], BF16, name="raw")
             nc.sync.dma_start(out=raw[:], in_=rows)
             words = raw[:].bitcast(F32)
@@ -101,6 +101,9 @@ def tile_gnn_layer_pb_t_kernel(
                     out=grouped_words[:, 2 * h : 2 * h + 2, :, :],
                     in_=flipped.rearrange("p j u r -> p j r u"),
                 )
+            return grouped
+
+        def quantise(operand, c, grouped):
             nc.vector.quantize_mx(
                 out=operand["codes"][:, c, :].bitcast(FP8X4),
                 scales=operand["scales"][:, c, :],
@@ -165,9 +168,6 @@ def tile_gnn_layer_pb_t_kernel(
 
         def turn_back(chunk, h):
             act = chunk["act"]
-            stage = None
-            if chunk["sample_block"] is not None:
-                stage = stages.tile([P, 2, DB], F32, name="stage")
             for j in range(2 * h, 2 * h + 2):
                 bank = rest.tile([P, CHUNK], F32, name="bank")
                 for o in range(BLOCKS):
@@ -177,15 +177,14 @@ def tile_gnn_layer_pb_t_kernel(
                 if chunk["sample_block"] is None:
                     nc.vector.tensor_copy(out=rf_to_bb[:, j, :], in_=bank[:])
                 else:
+                    s = chunk["sample_block"]
+                    stage = stages.tile([P, DB], F32, name="stage")
                     nc.vector.tensor_tensor(
-                        out=stage[:, j - 2 * h, :],
-                        in0=bank[:],
-                        in1=rf_to_bb[:, chunk["sample_block"], :],
-                        op=ALU.add,
+                        out=stage[:], in0=bank[:], in1=rf_to_bb[:, s, :], op=ALU.add
                     )
-            if chunk["sample_block"] is not None:
-                s, g0 = chunk["sample_block"], chunk["first_group"] + 2 * h
-                nc.sync.dma_start(out=out[s * P : (s + 1) * P, g0 : g0 + 2, :], in_=stage[:])
+                    nc.sync.dma_start(
+                        out=out[s * P : (s + 1) * P, chunk["first_group"] + j, :], in_=stage[:]
+                    )
 
         w_bb = new_operand("w_bb", 1)
         w_rf = new_operand("w_rf", DR // K_PASS)
@@ -234,15 +233,32 @@ def tile_gnn_layer_pb_t_kernel(
         def written_before(i):
             return min(len(passes), LEAD + i + i // 3)
 
-        done = 0
+        state = {"pending": None}
+
+        def quantise_pending():
+            if state["pending"] is not None:
+                quantise(*state["pending"])
+                state["pending"] = None
+
+        def prepare(k, scalar_helps=False):
+            operand, c, rows = passes[k]
+            grouped = regroup(rows, scalar_helps)
+            quantise_pending()
+            state["pending"] = (operand, c, grouped)
+
+        prepare(0, scalar_helps=True)
+        prepare(1, scalar_helps=True)
+        quantise_pending()
+        done = 2
         for i, chunk in enumerate(bb_chunks[:n_first] + [rf_chunk]):
             for k in range(done, written_before(i)):
-                prepare(*passes[k], scalar_helps=(k < 2))
+                prepare(k)
             done = written_before(i)
             sigmoid(chunk)
-        assert done >= 1 + n_first + len(rf_passes)
+        assert done > 1 + n_first + len(rf_passes)
         for k in range(done, len(passes)):
-            prepare(*passes[k])
+            prepare(k)
+        quantise_pending()
 
         for g, group in enumerate(groups):
             following = groups[g + 1] if g + 1 < len(groups) else []

@@ -20,10 +20,11 @@ K_PASS = P * PACK
 BLOCKS = 4
 CHUNK = BLOCKS * P
 HALF = BLOCKS // 2
+UNIT = CHUNK // 2
 
 GROUP_SIZES = (10, 5, 2)
 
-LEAD = 4
+LEAD = 7
 
 GUARD = 2.0 ** -60
 
@@ -35,8 +36,8 @@ def tile_gnn_layer_pb_t_kernel(
     with ExitStack() as ctx:
         consts = ctx.enter_context(tc.tile_pool(name="consts", bufs=1))
         keep = ctx.enter_context(tc.tile_pool(name="keep", bufs=1))
-        raws = ctx.enter_context(tc.tile_pool(name="raws", bufs=4))
-        groupeds = ctx.enter_context(tc.tile_pool(name="groupeds", bufs=4))
+        raws = ctx.enter_context(tc.tile_pool(name="raws", bufs=8))
+        groupeds = ctx.enter_context(tc.tile_pool(name="groupeds", bufs=8))
         acts = ctx.enter_context(tc.tile_pool(name="acts", bufs=13))
         stages = ctx.enter_context(tc.tile_pool(name="stages", bufs=8))
         front = ctx.enter_context(tc.psum_pool(name="front", bufs=4))
@@ -78,35 +79,30 @@ def tile_gnn_layer_pb_t_kernel(
             scales = keep.tile([P, passes, CHUNK], U8, name="scales_" + label, align_bytes=64)
             return {"codes": codes, "scales": scales, "passes": passes}
 
-        def regroup(rows, scalar_helps):
-            raw = raws.tile([P, BLOCKS, K_PASS], BF16, name="raw")
+        def regroup(rows, on_scalar):
+            raw = raws.tile([P, 2, K_PASS], BF16, name="raw")
             nc.sync.dma_start(out=raw[:], in_=rows)
             words = raw[:].bitcast(F32)
-            grouped = groupeds.tile([P, CHUNK * PACK], BF16, name="grouped", align_bytes=64)
-            grouped_words = grouped[:].bitcast(F32).rearrange(
-                "p (j r u) -> p j r u", j=BLOCKS, u=2
+            bank = rest.tile([P, CHUNK], F32, name="bank")
+            flipped = bank[:].rearrange("p (j u r) -> p j u r", j=2, u=2)
+            for j in range(2):
+                for u in range(2):
+                    nc.tensor.transpose(
+                        flipped[:, j, u, :], words[:, j, u * P : (u + 1) * P], ident[:]
+                    )
+            grouped = groupeds.tile([P, UNIT * PACK], BF16, name="grouped", align_bytes=64)
+            copy = nc.scalar.copy if on_scalar else nc.vector.tensor_copy
+            copy(
+                out=grouped[:].bitcast(F32).rearrange("p (j r u) -> p j r u", j=2, u=2),
+                in_=flipped.rearrange("p j u r -> p j r u"),
             )
-            for h in range(HALF):
-                bank = rest.tile([P, CHUNK], F32, name="bank")
-                flipped = bank[:].rearrange("p (j u r) -> p j u r", j=2, u=2)
-                for j in range(2):
-                    for u in range(2):
-                        nc.tensor.transpose(
-                            flipped[:, j, u, :],
-                            words[:, 2 * h + j, u * P : (u + 1) * P],
-                            ident[:],
-                        )
-                copy = nc.scalar.copy if scalar_helps and h == 1 else nc.vector.tensor_copy
-                copy(
-                    out=grouped_words[:, 2 * h : 2 * h + 2, :, :],
-                    in_=flipped.rearrange("p j u r -> p j r u"),
-                )
             return grouped
 
-        def quantise(operand, c, grouped):
+        def quantise(operand, c, h, grouped):
+            cols = slice(h * UNIT, (h + 1) * UNIT)
             nc.vector.quantize_mx(
-                out=operand["codes"][:, c, :].bitcast(FP8X4),
-                scales=operand["scales"][:, c, :],
+                out=operand["codes"][:, c, cols].bitcast(FP8X4),
+                scales=operand["scales"][:, c, cols],
                 in_=grouped[:],
             )
 
@@ -229,9 +225,15 @@ def tile_gnn_layer_pb_t_kernel(
         passes.extend([bb_pass(chunk) for chunk in bb_chunks[:n_first]])
         passes.extend(rf_passes)
         passes.extend([bb_pass(chunk) for chunk in bb_chunks[n_first:]])
+        units = []
+        for operand, c, rows in passes:
+            for h in range(HALF):
+                units.append((operand, c, h, rows[:, 2 * h : 2 * h + 2, :]))
+
+        n_first_units = HALF * (1 + n_first + len(rf_passes))
 
         def written_before(i):
-            return min(len(passes), LEAD + i + i // 3)
+            return min(n_first_units, LEAD + 8 * i // 3)
 
         state = {"pending": None}
 
@@ -240,36 +242,40 @@ def tile_gnn_layer_pb_t_kernel(
                 quantise(*state["pending"])
                 state["pending"] = None
 
-        def prepare(k, scalar_helps=False):
-            operand, c, rows = passes[k]
-            grouped = regroup(rows, scalar_helps)
+        def prepare(k, on_scalar=False):
+            operand, c, h, rows = units[k]
+            grouped = regroup(rows, on_scalar)
             quantise_pending()
-            state["pending"] = (operand, c, grouped)
+            state["pending"] = (operand, c, h, grouped)
 
-        prepare(0, scalar_helps=True)
-        prepare(1, scalar_helps=True)
+        for k in range(2 * HALF):
+            prepare(k, on_scalar=(k % 2 == 1))
         quantise_pending()
-        done = 2
+        done = 2 * HALF
         for i, chunk in enumerate(bb_chunks[:n_first] + [rf_chunk]):
             for k in range(done, written_before(i)):
                 prepare(k)
-            done = written_before(i)
+            done = max(done, written_before(i))
+            if done == n_first_units:
+                quantise_pending()
+            assert done == n_first_units or done > HALF * (i + 2)
             sigmoid(chunk)
-        assert done > 1 + n_first + len(rf_passes)
-        for k in range(done, len(passes)):
+        assert done == n_first_units
+        for k in range(done, len(units)):
             prepare(k)
         quantise_pending()
 
         for g, group in enumerate(groups):
             following = groups[g + 1] if g + 1 < len(groups) else []
+            assert len(following) < len(group)
             for chunk in group:
                 log(chunk)
             call_in_sigmoid_table()
             previous = None
             for i, chunk in enumerate(group):
                 tanh(chunk)
-                if i < len(following):
-                    sigmoid(following[i])
+                if 1 <= i <= len(following):
+                    sigmoid(following[i - 1])
                 for h in range(HALF):
                     times_z(chunk, h)
                     if previous is not None:

from contextlib import ExitStack

import concourse.mybir as mybir
from concourse.masks import make_identity

F32 = mybir.dt.float32
BF16 = mybir.dt.bfloat16
U32 = mybir.dt.uint32
U8 = mybir.dt.uint8
FP8X4 = mybir.dt.float8_e4m3fn_x4
ACT = mybir.ActivationFunctionType
ALU = mybir.AluOpType

B, G, DB, DR = 512, 16, 512, 1024
FLOPS = 2 * B * G * DB * DB + 2 * B * DR * DB

P = 128
PACK = 4
K_PASS = P * PACK
BLOCKS = 4
CHUNK = BLOCKS * P
HALF = BLOCKS // 2
UNIT = CHUNK // 2

GROUP_SIZES = (10, 5, 2)

LEAD = 7

GUARD = 2.0 ** -60


def tile_gnn_layer_pb_t_kernel(
    tc, BB_feature, RF_feature, W_bbbb, b_bbbb, W_rfbb, b_rfbb, out
):
    nc = tc.nc
    with ExitStack() as ctx:
        consts = ctx.enter_context(tc.tile_pool(name="consts", bufs=1))
        keep = ctx.enter_context(tc.tile_pool(name="keep", bufs=1))
        raws = ctx.enter_context(tc.tile_pool(name="raws", bufs=8))
        groupeds = ctx.enter_context(tc.tile_pool(name="groupeds", bufs=8))
        acts = ctx.enter_context(tc.tile_pool(name="acts", bufs=13))
        stages = ctx.enter_context(tc.tile_pool(name="stages", bufs=8))
        front = ctx.enter_context(tc.psum_pool(name="front", bufs=4))
        rest = ctx.enter_context(tc.psum_pool(name="rest", bufs=4))
        ctx.enter_context(tc.manual_schedule())

        ident = consts.tile([P, P], F32, name="ident")
        make_identity(nc, ident[:])
        guard = consts.tile([P, 1], F32, name="guard")
        nc.vector.memset(guard[:], GUARD)
        scratch = consts.tile([P, 1], F32, name="scratch")

        def call_in_sigmoid_table():
            nc.scalar.activation(out=scratch[:], in_=guard[:], func=ACT.Sigmoid)

        call_in_sigmoid_table()

        bias_rows = consts.tile([P, P], BF16, name="bias_rows")
        nc.vector.memset(bias_rows[:], 0.0)
        nc.sync.dma_start(
            out=bias_rows[0:BLOCKS, :], in_=b_bbbb.rearrange("(o p) -> o p", p=P)
        )
        nc.sync.dma_start(
            out=bias_rows[BLOCKS : 2 * BLOCKS, :], in_=b_rfbb.rearrange("(o p) -> o p", p=P)
        )
        bias_rows_f32 = consts.tile([P, P], F32, name="bias_rows_f32")
        nc.vector.tensor_copy(out=bias_rows_f32[:], in_=bias_rows[:])
        bias_bank = rest.tile([P, CHUNK], F32, name="bank")
        nc.tensor.transpose(bias_bank[:, 0:P], bias_rows_f32[:], ident[:])
        bias = consts.tile([P, 2 * BLOCKS], F32, name="bias")
        nc.vector.tensor_copy(out=bias[:], in_=bias_bank[:, 0 : 2 * BLOCKS])
        neg_bias = consts.tile([P, 2 * BLOCKS], F32, name="neg_bias")
        nc.vector.tensor_scalar_mul(out=neg_bias[:], in0=bias[:], scalar1=-1.0)

        rf_to_bb = consts.tile([P, BLOCKS, DB], F32, name="rf_to_bb")

        def new_operand(label, passes):
            codes = keep.tile([P, passes, CHUNK], U32, name="codes_" + label, align_bytes=64)
            scales = keep.tile([P, passes, CHUNK], U8, name="scales_" + label, align_bytes=64)
            return {"codes": codes, "scales": scales, "passes": passes}

        def regroup(rows, on_scalar):
            raw = raws.tile([P, 2, K_PASS], BF16, name="raw")
            nc.sync.dma_start(out=raw[:], in_=rows)
            words = raw[:].bitcast(F32)
            bank = rest.tile([P, CHUNK], F32, name="bank")
            flipped = bank[:].rearrange("p (j u r) -> p j u r", j=2, u=2)
            for j in range(2):
                for u in range(2):
                    nc.tensor.transpose(
                        flipped[:, j, u, :], words[:, j, u * P : (u + 1) * P], ident[:]
                    )
            grouped = groupeds.tile([P, UNIT * PACK], BF16, name="grouped", align_bytes=64)
            copy = nc.scalar.copy if on_scalar else nc.vector.tensor_copy
            copy(
                out=grouped[:].bitcast(F32).rearrange("p (j r u) -> p j r u", j=2, u=2),
                in_=flipped.rearrange("p j u r -> p j r u"),
            )
            return grouped

        def quantise(operand, c, h, grouped):
            cols = slice(h * UNIT, (h + 1) * UNIT)
            nc.vector.quantize_mx(
                out=operand["codes"][:, c, cols].bitcast(FP8X4),
                scales=operand["scales"][:, c, cols],
                in_=grouped[:],
            )

        def product(bank, chunk, o):
            w, x = chunk["w"], chunk["x"]
            cols = slice(o * P, (o + 1) * P)
            for c in range(x["passes"]):
                nc.tensor.matmul_mx(
                    out=bank[:],
                    lhsT=w["codes"][:, c, cols].bitcast(FP8X4),
                    lhsT_scale=w["scales"][:, c, cols],
                    rhs=x["codes"][:, c, :].bitcast(FP8X4),
                    rhs_scale=x["scales"][:, c, :],
                    start=(c == 0),
                    stop=(c == x["passes"] - 1),
                )

        def sigmoid(chunk):
            act = acts.tile([P, BLOCKS, CHUNK], F32, name="act")
            chunk["act"] = act
            for o in range(BLOCKS):
                bank = front.tile([P, CHUNK], F32, name="first")
                product(bank, chunk, o)
                col = chunk["bias"] + o
                nc.scalar.activation(
                    out=act[:, o, :],
                    in_=bank[:],
                    func=ACT.Sigmoid,
                    bias=neg_bias[:, col : col + 1],
                    scale=-1.0,
                )

        def log(chunk):
            act = chunk["act"]
            nc.scalar.activation(
                out=act[:], in_=act[:], func=ACT.Ln, bias=guard[:, 0:1], scale=1.0
            )

        def tanh(chunk):
            act = chunk["act"]
            for h in range(HALF):
                half = act[:, 2 * h : 2 * h + 2, :]
                nc.scalar.activation(out=half, in_=half, func=ACT.Tanh, scale=-1.0)

        def times_z(chunk, h):
            act = chunk["act"]
            for o in range(2 * h, 2 * h + 2):
                bank = rest.tile([P, CHUNK], F32, name="bank")
                product(bank, chunk, o)
                col = chunk["bias"] + o
                nc.vector.scalar_tensor_tensor(
                    out=act[:, o, :],
                    in0=bank[:],
                    scalar=bias[:, col : col + 1],
                    in1=act[:, o, :],
                    op0=ALU.add,
                    op1=ALU.mult,
                )

        def turn_back(chunk, h):
            act = chunk["act"]
            for j in range(2 * h, 2 * h + 2):
                bank = rest.tile([P, CHUNK], F32, name="bank")
                for o in range(BLOCKS):
                    nc.tensor.transpose(
                        bank[:, o * P : (o + 1) * P], act[:, o, j * P : (j + 1) * P], ident[:]
                    )
                if chunk["sample_block"] is None:
                    nc.vector.tensor_copy(out=rf_to_bb[:, j, :], in_=bank[:])
                else:
                    s = chunk["sample_block"]
                    stage = stages.tile([P, DB], F32, name="stage")
                    nc.vector.tensor_tensor(
                        out=stage[:], in0=bank[:], in1=rf_to_bb[:, s, :], op=ALU.add
                    )
                    nc.sync.dma_start(
                        out=out[s * P : (s + 1) * P, chunk["first_group"] + j, :], in_=stage[:]
                    )

        w_bb = new_operand("w_bb", 1)
        w_rf = new_operand("w_rf", DR // K_PASS)
        x_rf = new_operand("x_rf", DR // K_PASS)
        w_bb_rows = W_bbbb.rearrange("(j p) k -> p j k", p=P)
        w_rf_rows = W_rfbb.rearrange("(j p) k -> p j k", p=P)
        x_rf_rows = RF_feature.rearrange("(j p) k -> p j k", p=P)

        rf_chunk = {"x": x_rf, "w": w_rf, "bias": BLOCKS, "sample_block": None}
        rf_passes = []
        for c in range(DR // K_PASS):
            k_cols = slice(c * K_PASS, (c + 1) * K_PASS)
            rf_passes.append((w_rf, c, w_rf_rows[:, :, k_cols]))
            rf_passes.append((x_rf, c, x_rf_rows[:, :, k_cols]))

        bb_chunks = []
        for n in range(B * G // CHUNK):
            s, g0 = n // (G // BLOCKS), BLOCKS * (n % (G // BLOCKS))
            bb_chunks.append(
                {
                    "x": new_operand("x_bb%d" % n, 1),
                    "w": w_bb,
                    "bias": 0,
                    "sample_block": s,
                    "first_group": g0,
                }
            )

        def bb_pass(chunk):
            s, g0 = chunk["sample_block"], chunk["first_group"]
            return (chunk["x"], 0, BB_feature[s * P : (s + 1) * P, g0 : g0 + BLOCKS, :])

        n_first = GROUP_SIZES[0] - 1
        groups = [[rf_chunk] + bb_chunks[:n_first]]
        start = n_first
        for size in GROUP_SIZES[1:]:
            groups.append(bb_chunks[start : start + size])
            start += size
        assert start == len(bb_chunks)

        passes = [(w_bb, 0, w_bb_rows)]
        passes.extend([bb_pass(chunk) for chunk in bb_chunks[:n_first]])
        passes.extend(rf_passes)
        passes.extend([bb_pass(chunk) for chunk in bb_chunks[n_first:]])
        units = []
        for operand, c, rows in passes:
            for h in range(HALF):
                units.append((operand, c, h, rows[:, 2 * h : 2 * h + 2, :]))

        n_first_units = HALF * (1 + n_first + len(rf_passes))

        def written_before(i):
            return min(n_first_units, LEAD + 8 * i // 3)

        state = {"pending": None}

        def quantise_pending():
            if state["pending"] is not None:
                quantise(*state["pending"])
                state["pending"] = None

        def prepare(k, on_scalar=False):
            operand, c, h, rows = units[k]
            grouped = regroup(rows, on_scalar)
            quantise_pending()
            state["pending"] = (operand, c, h, grouped)

        for k in range(2 * HALF):
            prepare(k, on_scalar=(k % 2 == 1))
        quantise_pending()
        done = 2 * HALF
        for i, chunk in enumerate(bb_chunks[:n_first] + [rf_chunk]):
            for k in range(done, written_before(i)):
                prepare(k)
            done = max(done, written_before(i))
            if done == n_first_units:
                quantise_pending()
            assert done == n_first_units or done > HALF * (i + 2)
            sigmoid(chunk)
        assert done == n_first_units
        for k in range(done, len(units)):
            prepare(k)
        quantise_pending()

        for g, group in enumerate(groups):
            following = groups[g + 1] if g + 1 < len(groups) else []
            assert len(following) < len(group)
            for chunk in group:
                log(chunk)
            call_in_sigmoid_table()
            previous = None
            for i, chunk in enumerate(group):
                tanh(chunk)
                if 1 <= i <= len(following):
                    sigmoid(following[i - 1])
                for h in range(HALF):
                    times_z(chunk, h)
                    if previous is not None:
                        turn_back(previous, h)
                previous = chunk
            for h in range(HALF):
                turn_back(previous, h)
